import numpy as np
import ml_dtypes


def mxq(x, axis, fmt="e4m3"):
    dtype, down = {"e4m3": (ml_dtypes.float8_e4m3fn, 7), "e5m2": (ml_dtypes.float8_e5m2, 14)}[fmt]
    v = np.moveaxis(np.asarray(x, np.float32).astype(ml_dtypes.bfloat16).astype(np.float64), axis, -1)
    blocks = v.reshape(v.shape[:-1] + (-1, 32))
    amax = np.abs(blocks).max(-1, keepdims=True)
    byte = np.maximum(np.where(amax > 0, np.frexp(amax)[1] - 1 + 127, 0) - down, 1)
    scale = np.exp2(byte - 127.0)
    codes = (blocks / scale).astype(np.float32).astype(dtype).astype(np.float64)
    return np.moveaxis((codes * scale).reshape(v.shape), -1, axis)


WIDE = False


def mx_kscale(k):
    if not WIDE:
        return np.ones(k)
    levels = np.array([10, -10, 5, -5, 0])
    a = np.random.permutation(np.resize(levels, k // 512 * 4)).reshape(k // 512, 4)
    idx = np.arange(k)
    return np.exp2(a[idx // 512, idx % 128 // 32])


BF16 = ml_dtypes.bfloat16


def bf(x):
    return np.asarray(x, np.float32).astype(BF16)


def f64(x):
    return np.asarray(x).astype(np.float64)


B, D, K = 5120, 512, 2


def setup_inputs():
    s = mx_kscale(D)
    x = np.random.standard_normal((B, D, K)) * s[None, :, None]
    mu = np.random.standard_normal((D, K)) * 0.3 * s[:, None]
    w = (np.eye(D)[None] + np.random.standard_normal((K, D, D)) * 0.7 / np.sqrt(D)) / s[None, None, :]
    return {"x": bf(x), "mu_track": bf(mu), "Std_inv_track": bf(w)}


def reference(x, mu_track, Std_inv_track):
    x_cnt = f64(x) - f64(mu_track)[None]
    xq = mxq(x_cnt, 1, "e4m3")
    wq = mxq(f64(Std_inv_track), 2, "e4m3")
    z = wq @ xq.transpose(2, 1, 0)
    return z.transpose(2, 1, 0)

@@ -1,0 +1,197 @@
+from contextlib import ExitStack
+
+import concourse.mybir as mybir
+from concourse.masks import make_identity
+
+F32 = mybir.dt.float32
+BF16 = mybir.dt.bfloat16
+U32 = mybir.dt.uint32
+U8 = mybir.dt.uint8
+FP8X4 = mybir.dt.float8_e4m3fn_x4
+
+P = 128
+B, D, K = 5120, 512, 2
+T = D // P
+NT = B // P
+FLOPS = 2 * B * D * D * K
+
+X_CHUNKS = [1, 1, 2, 4, 4, 4, 8, 8, 8]
+O_CHUNKS = [4, 4, 4, 4, 4, 4, 4, 4, 4, 2, 1, 1]
+O_MAX = 4
+
+
+def tile_clusternorm1dv3_t_kernel(tc, x, mu_track, Std_inv_track, out):
+    nc = tc.nc
+    assert sum(X_CHUNKS) == NT and sum(O_CHUNKS) == NT
+
+    xv = x.rearrange("(p j) e k -> p j (e k)", j=NT)
+    ov = out.rearrange("(p j) d k -> p j (d k)", j=NT)
+    wv = Std_inv_track.rearrange("k (c p) e -> k p c e", p=P)
+    muv = mu_track.rearrange("(t p) k -> p t k", p=P)
+
+    with ExitStack() as ctx:
+        ctx.enter_context(tc.manual_schedule())
+        keep = ctx.enter_context(tc.tile_pool(name="keep", bufs=1))
+        gpool = ctx.enter_context(tc.tile_pool(name="gpool", bufs=4))
+        cpool = ctx.enter_context(tc.tile_pool(name="cpool", bufs=3))
+        opool = ctx.enter_context(tc.tile_pool(name="opool", bufs=6))
+        psum_t = ctx.enter_context(tc.psum_pool(name="psum_t", bufs=4))
+        psum_o = ctx.enter_context(tc.psum_pool(name="psum_o", bufs=4))
+
+        mu_sb = keep.tile([P, T, K], BF16, name="mu_sb")
+        nc.scalar.dma_start(out=mu_sb[:], in_=muv)
+
+        x_tiles = []
+        x_loads = []
+        j0 = 0
+        for ci, n in enumerate(X_CHUNKS):
+            x_sb = keep.tile([P, n, D * K], BF16, name="x_sb%d" % ci)
+            x_loads.append((x_sb, j0, n))
+            for jj in range(n):
+                x_tiles.append((x_sb, jj))
+            j0 += n
+        w_sb = [keep.tile([P, T, D], BF16, name="w_sb%d" % k) for k in range(K)]
+
+        def load_x(ci):
+            x_sb, a, n = x_loads[ci]
+            nc.sync.dma_start(out=x_sb[:], in_=xv[:, a : a + n, :])
+
+        load_x(0)
+        nc.sync.dma_start(out=w_sb[0][:], in_=wv[0])
+        load_x(1)
+        nc.sync.dma_start(out=w_sb[1][:], in_=wv[1])
+        for ci in range(2, len(X_CHUNKS)):
+            load_x(ci)
+
+        ident_f = keep.tile([P, P], F32, name="ident_f")
+        make_identity(nc, ident_f[:])
+        ident_b = keep.tile([P, P], BF16, name="ident_b")
+        make_identity(nc, ident_b[:])
+
+        w_grp = [keep.tile([P, D, T], BF16, name="w_grp%d" % k, align_bytes=64) for k in range(K)]
+        w_codes = keep.tile([P, K, D], U32, name="w_codes", align_bytes=64)
+        w_scales = keep.tile([P, K, D], U8, name="w_scales", align_bytes=64)
+
+        mu_b = mu_sb[:].rearrange("p t k -> p k t").unsqueeze(2).to_broadcast([P, K, P, T])
+
+        xt_of = {}
+        xg_of = {}
+        xq_of = {}
+
+        def stage_a(j):
+            x_sb, jj = x_tiles[j]
+            words = x_sb[:].bitcast(F32)
+            xt = psum_t.tile([P, T, P], F32, name="xt", tag="xt")
+            for t in range(T):
+                nc.tensor.transpose(xt[:, t, :], words[:, jj, t * P : (t + 1) * P], ident_f[:])
+            xt_of[j] = xt
+
+        def stage_b(j):
+            xg = gpool.tile([P, K, P, T], BF16, name="xg", tag="xg", align_bytes=64)
+            nc.vector.tensor_tensor(
+                out=xg[:],
+                in0=xt_of[j][:].bitcast(BF16).rearrange("p t (b k) -> p k b t", k=K),
+                in1=mu_b,
+                op=mybir.AluOpType.subtract,
+            )
+            xg_of[j] = xg
+
+        def stage_c(j):
+            xc = cpool.tile([P, K * P], U32, name="xc", tag="xc", align_bytes=64)
+            xs = cpool.tile([P, K * P], U8, name="xs", tag="xs", align_bytes=64)
+            nc.vector.quantize_mx(
+                out=xc[:].bitcast(FP8X4),
+                scales=xs[:],
+                in_=xg_of[j][:].rearrange("p k b t -> p (k b t)"),
+            )
+            xq_of[j] = (xc, xs)
+
+        o_state = {"chunk": 0, "fill": 0, "start": 0, "tile": None}
+
+        def stage_d_e(j):
+            xc, xs = xq_of[j]
+            H = D // 2
+            po = [psum_o.tile([P, K, H], F32, name="po", tag="po") for h in range(2)]
+            for k in range(K):
+                for h in range(2):
+                    nc.tensor.matmul_mx(
+                        out=po[h][:, k, :],
+                        lhsT=xc[:, k * P : (k + 1) * P].bitcast(FP8X4),
+                        lhsT_scale=xs[:, k * P : (k + 1) * P],
+                        rhs=w_codes[:, k, h * H : (h + 1) * H].bitcast(FP8X4),
+                        rhs_scale=w_scales[:, k, h * H : (h + 1) * H],
+                        start=True,
+                        stop=True,
+                    )
+            if o_state["fill"] == 0:
+                o_state["tile"] = opool.tile([P, O_MAX, D * K], F32, name="o_sb", tag="o_sb")
+            o_sb = o_state["tile"]
+            jj = o_state["fill"]
+            for h in range(2):
+                nc.scalar.copy(
+                    out=o_sb[:, jj, h * H * K : (h + 1) * H * K].rearrange("p (d k) -> p d k", k=K),
+                    in_=po[h][:].rearrange("p k d -> p d k"),
+                )
+            o_state["fill"] += 1
+            n = O_CHUNKS[o_state["chunk"]]
+            if o_state["fill"] == n:
+                a = o_state["start"]
+                nc.sync.dma_start(out=ov[:, a : a + n, :], in_=o_sb[:, 0:n, :])
+                o_state["start"] = a + n
+                o_state["chunk"] += 1
+                o_state["fill"] = 0
+
+        def w_transposes(k):
+            banks = []
+            for cp in range(2):
+                wt = psum_o.tile([P, 2, T, P], BF16, name="wt", tag="po")
+                for c2 in range(2):
+                    for t in range(T):
+                        nc.tensor.transpose(
+                            wt[:, c2, t, :], w_sb[k][:, 2 * cp + c2, t * P : (t + 1) * P], ident_b[:]
+                        )
+                banks.append(wt)
+            return banks
+
+        def w_copy(k, cp, wt, engine):
+            dst = w_grp[k][:, 2 * cp * P : 2 * (cp + 1) * P, :].rearrange("p (c d) t -> p c d t", c=2)
+            src = wt[:].rearrange("p c t d -> p c d t")
+            if engine == "v":
+                nc.vector.tensor_copy(out=dst, in_=src)
+            else:
+                nc.scalar.copy(out=dst, in_=src)
+
+        def w_quant(k):
+            nc.vector.quantize_mx(
+                out=w_codes[:, k, :].bitcast(FP8X4),
+                scales=w_scales[:, k, :],
+                in_=w_grp[k][:].rearrange("p d t -> p (d t)"),
+            )
+
+        stage_a(0)
+        wt0 = w_transposes(0)
+        stage_b(0)
+        w_copy(0, 0, wt0[0], "v")
+        w_copy(0, 1, wt0[1], "s")
+        stage_a(1)
+        wt1 = w_transposes(1)
+        stage_b(1)
+        w_copy(1, 0, wt1[0], "s")
+        w_copy(1, 1, wt1[1], "s")
+        w_quant(0)
+        stage_a(2)
+        stage_b(2)
+        w_quant(1)
+        stage_a(3)
+        stage_a(4)
+        stage_c(0)
+        stage_d_e(0)
+        stage_c(1)
+        stage_d_e(1)
+        for i in range(2, NT):
+            if i + 3 < NT:
+                stage_a(i + 3)
+            if i + 1 < NT:
+                stage_b(i + 1)
+            stage_c(i)
+            stage_d_e(i)

@@ -8,16 +8,20 @@ BF16 = mybir.dt.bfloat16
 U32 = mybir.dt.uint32
 U8 = mybir.dt.uint8
 FP8X4 = mybir.dt.float8_e4m3fn_x4
+ALU = mybir.AluOpType
 
 P = 128
 B, D, K = 5120, 512, 2
 T = D // P
+H = D // 2
 NT = B // P
+NP = NT // 2
 FLOPS = 2 * B * D * D * K
 
 X_CHUNKS = [1, 1, 2, 4, 4, 4, 8, 8, 8]
-O_CHUNKS = [4, 4, 4, 4, 4, 4, 4, 4, 4, 2, 1, 1]
+O_CHUNKS = [4, 4, 4, 4, 4, 4, 4, 4, 4, 2, 2]
 O_MAX = 4
+O_BUFS = 6
 
 
 def tile_clusternorm1dv3_t_kernel(tc, x, mu_track, Std_inv_track, out):
@@ -32,9 +36,10 @@ def tile_clusternorm1dv3_t_kernel(tc, x, mu_track, Std_inv_track, out):
     with ExitStack() as ctx:
         ctx.enter_context(tc.manual_schedule())
         keep = ctx.enter_context(tc.tile_pool(name="keep", bufs=1))
-        gpool = ctx.enter_context(tc.tile_pool(name="gpool", bufs=4))
+        rpool = ctx.enter_context(tc.tile_pool(name="rpool", bufs=2))
+        gpool = ctx.enter_context(tc.tile_pool(name="gpool", bufs=3))
         cpool = ctx.enter_context(tc.tile_pool(name="cpool", bufs=3))
-        opool = ctx.enter_context(tc.tile_pool(name="opool", bufs=6))
+        opool = ctx.enter_context(tc.tile_pool(name="opool", bufs=O_BUFS))
         psum_t = ctx.enter_context(tc.psum_pool(name="psum_t", bufs=4))
         psum_o = ctx.enter_context(tc.psum_pool(name="psum_o", bufs=4))
 
@@ -57,8 +62,8 @@ def tile_clusternorm1dv3_t_kernel(tc, x, mu_track, Std_inv_track, out):
             nc.sync.dma_start(out=x_sb[:], in_=xv[:, a : a + n, :])
 
         load_x(0)
-        nc.sync.dma_start(out=w_sb[0][:], in_=wv[0])
         load_x(1)
+        nc.sync.dma_start(out=w_sb[0][:], in_=wv[0])
         nc.sync.dma_start(out=w_sb[1][:], in_=wv[1])
         for ci in range(2, len(X_CHUNKS)):
             load_x(ci)
@@ -72,13 +77,15 @@ def tile_clusternorm1dv3_t_kernel(tc, x, mu_track, Std_inv_track, out):
         w_codes = keep.tile([P, K, D], U32, name="w_codes", align_bytes=64)
         w_scales = keep.tile([P, K, D], U8, name="w_scales", align_bytes=64)
 
-        mu_b = mu_sb[:].rearrange("p t k -> p k t").unsqueeze(2).to_broadcast([P, K, P, T])
+        mu_kbt = mu_sb[:].rearrange("p t k -> p k t").unsqueeze(2).to_broadcast([P, K, P, T])
+        mu_tbk = mu_sb[:].unsqueeze(2).to_broadcast([P, T, P, K])
 
         xt_of = {}
+        xr_of = {}
         xg_of = {}
         xq_of = {}
 
-        def stage_a(j):
+        def transposes(j):
             x_sb, jj = x_tiles[j]
             words = x_sb[:].bitcast(F32)
             xt = psum_t.tile([P, T, P], F32, name="xt", tag="xt")
@@ -86,60 +93,87 @@ def tile_clusternorm1dv3_t_kernel(tc, x, mu_track, Std_inv_track, out):
                 nc.tensor.transpose(xt[:, t, :], words[:, jj, t * P : (t + 1) * P], ident_f[:])
             xt_of[j] = xt
 
-        def stage_b(j):
-            xg = gpool.tile([P, K, P, T], BF16, name="xg", tag="xg", align_bytes=64)
-            nc.vector.tensor_tensor(
-                out=xg[:],
-                in0=xt_of[j][:].bitcast(BF16).rearrange("p t (b k) -> p k b t", k=K),
-                in1=mu_b,
-                op=mybir.AluOpType.subtract,
-            )
-            xg_of[j] = xg
+        def pair_tile(n):
+            if n not in xg_of:
+                xg_of[n] = gpool.tile([P, 2, K, P, T], BF16, name="xg", tag="xg", align_bytes=64)
+            return xg_of[n]
 
-        def stage_c(j):
-            xc = cpool.tile([P, K * P], U32, name="xc", tag="xc", align_bytes=64)
-            xs = cpool.tile([P, K * P], U8, name="xs", tag="xs", align_bytes=64)
+        def centre_and_regroup(j):
+            nc.vector.tensor_tensor(
+                out=pair_tile(j // 2)[:, 1],
+                in0=xt_of[j][:].bitcast(BF16).rearrange("p t (b k) -> p k b t", k=K),
+                in1=mu_kbt,
+                op=ALU.subtract,
+            )
+
+        def centre_only(j):
+            xr = rpool.tile([P, T, P, K], BF16, name="xr", tag="xr")
+            nc.vector.tensor_tensor(
+                out=xr[:],
+                in0=xt_of[j][:].bitcast(BF16).rearrange("p t (b k) -> p t b k", k=K),
+                in1=mu_tbk,
+                op=ALU.subtract,
+            )
+            xr_of[j] = xr
+
+        def regroup(j):
+            dst = pair_tile(j // 2)[:, 0]
+            src = xr_of[j][:].rearrange("p t b k -> p k b t")
+            nc.gpsimd.tensor_scalar(out=dst, in0=src, scalar1=1.0, scalar2=0.0, op0=ALU.mult, op1=ALU.add)
+
+        def quantise(n):
+            xc = cpool.tile([P, 2 * K * P], U32, name="xc", tag="xc", align_bytes=64)
+            xs = cpool.tile([P, 2 * K * P], U8, name="xs", tag="xs", align_bytes=64)
             nc.vector.quantize_mx(
                 out=xc[:].bitcast(FP8X4),
                 scales=xs[:],
-                in_=xg_of[j][:].rearrange("p k b t -> p (k b t)"),
+                in_=xg_of[n][:].rearrange("p s k b t -> p (s k b t)"),
             )
-            xq_of[j] = (xc, xs)
+            xq_of[n] = (xc, xs)
 
         o_state = {"chunk": 0, "fill": 0, "start": 0, "tile": None}
 
-        def stage_d_e(j):
-            xc, xs = xq_of[j]
-            H = D // 2
-            po = [psum_o.tile([P, K, H], F32, name="po", tag="po") for h in range(2)]
-            for k in range(K):
+        def multiply(n):
+            xc, xs = xq_of[n]
+            banks = []
+            for s in range(2):
+                po = [psum_o.tile([P, K, H], F32, name="po", tag="po") for h in range(2)]
+                for k in range(K):
+                    c0 = (s * K + k) * P
+                    for h in range(2):
+                        nc.tensor.matmul_mx(
+                            out=po[h][:, k, :],
+                            lhsT=xc[:, c0 : c0 + P].bitcast(FP8X4),
+                            lhsT_scale=xs[:, c0 : c0 + P],
+                            rhs=w_codes[:, k, h * H : (h + 1) * H].bitcast(FP8X4),
+                            rhs_scale=w_scales[:, k, h * H : (h + 1) * H],
+                            start=True,
+                            stop=True,
+                        )
+                banks.append(po)
+            return banks
+
+        def drain(banks, engines):
+            for s in range(2):
+                if o_state["fill"] == 0:
+                    o_state["tile"] = opool.tile([P, O_MAX, D * K], F32, name="o_sb", tag="o_sb")
+                o_sb = o_state["tile"]
+                jj = o_state["fill"]
                 for h in range(2):
-                    nc.tensor.matmul_mx(
-                        out=po[h][:, k, :],
-                        lhsT=xc[:, k * P : (k + 1) * P].bitcast(FP8X4),
-                        lhsT_scale=xs[:, k * P : (k + 1) * P],
-                        rhs=w_codes[:, k, h * H : (h + 1) * H].bitcast(FP8X4),
-                        rhs_scale=w_scales[:, k, h * H : (h + 1) * H],
-                        start=True,
-                        stop=True,
-                    )
-            if o_state["fill"] == 0:
-                o_state["tile"] = opool.tile([P, O_MAX, D * K], F32, name="o_sb", tag="o_sb")
-            o_sb = o_state["tile"]
-            jj = o_state["fill"]
-            for h in range(2):
-                nc.scalar.copy(
-                    out=o_sb[:, jj, h * H * K : (h + 1) * H * K].rearrange("p (d k) -> p d k", k=K),
-                    in_=po[h][:].rearrange("p k d -> p d k"),
-                )
-            o_state["fill"] += 1
-            n = O_CHUNKS[o_state["chunk"]]
-            if o_state["fill"] == n:
-                a = o_state["start"]
-                nc.sync.dma_start(out=ov[:, a : a + n, :], in_=o_sb[:, 0:n, :])
-                o_state["start"] = a + n
-                o_state["chunk"] += 1
-                o_state["fill"] = 0
+                    dst = o_sb[:, jj, h * H * K : (h + 1) * H * K].rearrange("p (d k) -> p d k", k=K)
+                    src = banks[s][h][:].rearrange("p k d -> p d k")
+                    if engines[s] == "v":
+                        nc.vector.tensor_copy(out=dst, in_=src)
+                    else:
+                        nc.scalar.copy(out=dst, in_=src)
+                o_state["fill"] += 1
+                n = O_CHUNKS[o_state["chunk"]]
+                if o_state["fill"] == n:
+                    a = o_state["start"]
+                    nc.sync.dma_start(out=ov[:, a : a + n, :], in_=o_sb[:, 0:n, :])
+                    o_state["start"] = a + n
+                    o_state["chunk"] += 1
+                    o_state["fill"] = 0
 
         def w_transposes(k):
             banks = []
@@ -168,30 +202,34 @@ def tile_clusternorm1dv3_t_kernel(tc, x, mu_track, Std_inv_track, out):
                 in_=w_grp[k][:].rearrange("p d t -> p (d t)"),
             )
 
-        stage_a(0)
+        transposes(0)
+        transposes(1)
+        centre_only(0)
+        regroup(0)
         wt0 = w_transposes(0)
-        stage_b(0)
+        centre_and_regroup(1)
         w_copy(0, 0, wt0[0], "v")
         w_copy(0, 1, wt0[1], "s")
-        stage_a(1)
         wt1 = w_transposes(1)
-        stage_b(1)
         w_copy(1, 0, wt1[0], "s")
-        w_copy(1, 1, wt1[1], "s")
+        w_copy(1, 1, wt1[1], "v")
+        transposes(2)
+        transposes(3)
         w_quant(0)
-        stage_a(2)
-        stage_b(2)
+        centre_only(2)
+        regroup(2)
         w_quant(1)
-        stage_a(3)
-        stage_a(4)
-        stage_c(0)
-        stage_d_e(0)
-        stage_c(1)
-        stage_d_e(1)
-        for i in range(2, NT):
-            if i + 3 < NT:
-                stage_a(i + 3)
-            if i + 1 < NT:
-                stage_b(i + 1)
-            stage_c(i)
-            stage_d_e(i)
+        transposes(4)
+        transposes(5)
+        quantise(0)
+        drain(multiply(0), "ss")
+        for n in range(1, NP):
+            centre_and_regroup(2 * n + 1)
+            if n + 1 < NP:
+                centre_only(2 * n + 2)
+                regroup(2 * n + 2)
+            if n + 2 < NP:
+                transposes(2 * n + 4)
+                transposes(2 * n + 5)
+            quantise(n)
+            drain(multiply(n), "sv" if n == NP - 1 else "ss")

@@ -18,10 +18,10 @@ NT = B // P
 NP = NT // 2
 FLOPS = 2 * B * D * D * K
 
-X_CHUNKS = [1, 1, 2, 4, 4, 4, 8, 8, 8]
-O_CHUNKS = [4, 4, 4, 4, 4, 4, 4, 4, 4, 2, 2]
-O_MAX = 4
-O_BUFS = 6
+X_CHUNKS = [1, 1, 2, 4, 8, 8, 16]
+O_CHUNKS = [8, 8, 8, 8, 4, 4]
+O_MAX = 8
+O_BUFS = 3
 
 
 def tile_clusternorm1dv3_t_kernel(tc, x, mu_track, Std_inv_track, out):
@@ -30,8 +30,8 @@ def tile_clusternorm1dv3_t_kernel(tc, x, mu_track, Std_inv_track, out):
 
     xv = x.rearrange("(p j) e k -> p j (e k)", j=NT)
     ov = out.rearrange("(p j) d k -> p j (d k)", j=NT)
-    wv = Std_inv_track.rearrange("k (c p) e -> k p c e", p=P)
-    muv = mu_track.rearrange("(t p) k -> p t k", p=P)
+    wv = Std_inv_track.rearrange("k (p c) e -> k p c e", c=T)
+    muv = mu_track.rearrange("(t p) k -> t (p k)", t=T)
 
     with ExitStack() as ctx:
         ctx.enter_context(tc.manual_schedule())
@@ -43,8 +43,9 @@ def tile_clusternorm1dv3_t_kernel(tc, x, mu_track, Std_inv_track, out):
         psum_t = ctx.enter_context(tc.psum_pool(name="psum_t", bufs=4))
         psum_o = ctx.enter_context(tc.psum_pool(name="psum_o", bufs=4))
 
-        mu_sb = keep.tile([P, T, K], BF16, name="mu_sb")
-        nc.scalar.dma_start(out=mu_sb[:], in_=muv)
+        mu_raw = keep.tile([P, P], F32, name="mu_raw")
+        nc.vector.memset(mu_raw[:], 0.0)
+        nc.scalar.dma_start(out=mu_raw[0:T, :].bitcast(BF16), in_=muv)
 
         x_tiles = []
         x_loads = []
@@ -77,8 +78,13 @@ def tile_clusternorm1dv3_t_kernel(tc, x, mu_track, Std_inv_track, out):
         w_codes = keep.tile([P, K, D], U32, name="w_codes", align_bytes=64)
         w_scales = keep.tile([P, K, D], U8, name="w_scales", align_bytes=64)
 
-        mu_kbt = mu_sb[:].rearrange("p t k -> p k t").unsqueeze(2).to_broadcast([P, K, P, T])
-        mu_tbk = mu_sb[:].unsqueeze(2).to_broadcast([P, T, P, K])
+        mt = psum_t.tile([P, P], F32, name="mt", tag="xt")
+        nc.tensor.transpose(mt[:], mu_raw[:], ident_f[:])
+        mu_w = keep.tile([P, T], F32, name="mu_w")
+        nc.vector.tensor_copy(out=mu_w[:], in_=mt[:, 0:T])
+        mu_sb = mu_w[:].bitcast(BF16).rearrange("p (t k) -> p t k", k=K)
+        mu_kbt = mu_sb.rearrange("p t k -> p k t").unsqueeze(2).to_broadcast([P, K, P, T])
+        mu_tbk = mu_sb.unsqueeze(2).to_broadcast([P, T, P, K])
 
         xt_of = {}
         xr_of = {}
@@ -188,8 +194,8 @@ def tile_clusternorm1dv3_t_kernel(tc, x, mu_track, Std_inv_track, out):
             return banks
 
         def w_copy(k, cp, wt, engine):
-            dst = w_grp[k][:, 2 * cp * P : 2 * (cp + 1) * P, :].rearrange("p (c d) t -> p c d t", c=2)
-            src = wt[:].rearrange("p c t d -> p c d t")
+            dst = w_grp[k][:].rearrange("p (q a c) t -> p q a (c t)", a=2, c=2)[:, :, cp, :]
+            src = wt[:].rearrange("p c t q -> p q (c t)")
             if engine == "v":
                 nc.vector.tensor_copy(out=dst, in_=src)
             else:
@@ -209,10 +215,10 @@ def tile_clusternorm1dv3_t_kernel(tc, x, mu_track, Std_inv_track, out):
         wt0 = w_transposes(0)
         centre_and_regroup(1)
         w_copy(0, 0, wt0[0], "v")
-        w_copy(0, 1, wt0[1], "s")
+        w_copy(0, 1, wt0[1], "v")
         wt1 = w_transposes(1)
         w_copy(1, 0, wt1[0], "s")
-        w_copy(1, 1, wt1[1], "v")
+        w_copy(1, 1, wt1[1], "s")
         transposes(2)
         transposes(3)
         w_quant(0)

@@ -19,9 +19,9 @@ NP = NT // 2
 FLOPS = 2 * B * D * D * K
 
 X_CHUNKS = [1, 1, 2, 4, 8, 8, 16]
-O_CHUNKS = [8, 8, 8, 8, 4, 4]
-O_MAX = 8
-O_BUFS = 3
+O_CHUNKS = [4, 4, 4, 4, 4, 4, 4, 4, 4, 2, 2]
+O_MAX = 4
+O_BUFS = 6
 
 
 def tile_clusternorm1dv3_t_kernel(tc, x, mu_track, Std_inv_track, out):
@@ -44,8 +44,7 @@ def tile_clusternorm1dv3_t_kernel(tc, x, mu_track, Std_inv_track, out):
         psum_o = ctx.enter_context(tc.psum_pool(name="psum_o", bufs=4))
 
         mu_raw = keep.tile([P, P], F32, name="mu_raw")
-        nc.vector.memset(mu_raw[:], 0.0)
-        nc.scalar.dma_start(out=mu_raw[0:T, :].bitcast(BF16), in_=muv)
+        nc.gpsimd.memset(mu_raw[:], 0.0)
 
         x_tiles = []
         x_loads = []
@@ -63,6 +62,7 @@ def tile_clusternorm1dv3_t_kernel(tc, x, mu_track, Std_inv_track, out):
             nc.sync.dma_start(out=x_sb[:], in_=xv[:, a : a + n, :])
 
         load_x(0)
+        nc.sync.dma_start(out=mu_raw[0:T, :].bitcast(BF16), in_=muv)
         load_x(1)
         nc.sync.dma_start(out=w_sb[0][:], in_=wv[0])
         nc.sync.dma_start(out=w_sb[1][:], in_=wv[1])

@@ -34,7 +34,6 @@ def tile_clusternorm1dv3_t_kernel(tc, x, mu_track, Std_inv_track, out):
     muv = mu_track.rearrange("(t p) k -> t (p k)", t=T)
 
     with ExitStack() as ctx:
-        ctx.enter_context(tc.manual_schedule())
         keep = ctx.enter_context(tc.tile_pool(name="keep", bufs=1))
         rpool = ctx.enter_context(tc.tile_pool(name="rpool", bufs=2))
         gpool = ctx.enter_context(tc.tile_pool(name="gpool", bufs=3))

@@ -19,9 +19,8 @@ NP = NT // 2
 FLOPS = 2 * B * D * D * K
 
 X_CHUNKS = [1, 1, 2, 4, 8, 8, 16]
-O_CHUNKS = [4, 4, 4, 4, 4, 4, 4, 4, 4, 2, 2]
-O_MAX = 4
-O_BUFS = 6
+O_CHUNKS = [8, 8, 8, 4, 4, 4, 4]
+O_RING = 24
 
 
 def tile_clusternorm1dv3_t_kernel(tc, x, mu_track, Std_inv_track, out):
@@ -34,11 +33,11 @@ def tile_clusternorm1dv3_t_kernel(tc, x, mu_track, Std_inv_track, out):
     muv = mu_track.rearrange("(t p) k -> t (p k)", t=T)
 
     with ExitStack() as ctx:
+        ctx.enter_context(tc.manual_schedule())
         keep = ctx.enter_context(tc.tile_pool(name="keep", bufs=1))
         rpool = ctx.enter_context(tc.tile_pool(name="rpool", bufs=2))
         gpool = ctx.enter_context(tc.tile_pool(name="gpool", bufs=3))
         cpool = ctx.enter_context(tc.tile_pool(name="cpool", bufs=3))
-        opool = ctx.enter_context(tc.tile_pool(name="opool", bufs=O_BUFS))
         psum_t = ctx.enter_context(tc.psum_pool(name="psum_t", bufs=4))
         psum_o = ctx.enter_context(tc.psum_pool(name="psum_o", bufs=4))
 
@@ -136,7 +135,8 @@ def tile_clusternorm1dv3_t_kernel(tc, x, mu_track, Std_inv_track, out):
             )
             xq_of[n] = (xc, xs)
 
-        o_state = {"chunk": 0, "fill": 0, "start": 0, "tile": None}
+        o_ring = keep.tile([P, O_RING, D * K], F32, name="o_ring")
+        o_state = {"chunk": 0, "fill": 0, "start": 0}
 
         def multiply(n):
             xc, xs = xq_of[n]
@@ -160,12 +160,10 @@ def tile_clusternorm1dv3_t_kernel(tc, x, mu_track, Std_inv_track, out):
 
         def drain(banks, engines):
             for s in range(2):
-                if o_state["fill"] == 0:
-                    o_state["tile"] = opool.tile([P, O_MAX, D * K], F32, name="o_sb", tag="o_sb")
-                o_sb = o_state["tile"]
-                jj = o_state["fill"]
+                pos = o_state["start"] % O_RING
+                jj = pos + o_state["fill"]
                 for h in range(2):
-                    dst = o_sb[:, jj, h * H * K : (h + 1) * H * K].rearrange("p (d k) -> p d k", k=K)
+                    dst = o_ring[:, jj, h * H * K : (h + 1) * H * K].rearrange("p (d k) -> p d k", k=K)
                     src = banks[s][h][:].rearrange("p k d -> p d k")
                     if engines[s] == "v":
                         nc.vector.tensor_copy(out=dst, in_=src)
@@ -175,7 +173,7 @@ def tile_clusternorm1dv3_t_kernel(tc, x, mu_track, Std_inv_track, out):
                 n = O_CHUNKS[o_state["chunk"]]
                 if o_state["fill"] == n:
                     a = o_state["start"]
-                    nc.sync.dma_start(out=ov[:, a : a + n, :], in_=o_sb[:, 0:n, :])
+                    nc.sync.dma_start(out=ov[:, a : a + n, :], in_=o_ring[:, pos : pos + n, :])
                     o_state["start"] = a + n
                     o_state["chunk"] += 1
                     o_state["fill"] = 0

from contextlib import ExitStack

import concourse.mybir as mybir
from concourse.masks import make_identity

F32 = mybir.dt.float32
BF16 = mybir.dt.bfloat16
U32 = mybir.dt.uint32
U8 = mybir.dt.uint8
FP8X4 = mybir.dt.float8_e4m3fn_x4
ALU = mybir.AluOpType

P = 128
B, D, K = 5120, 512, 2
T = D // P
H = D // 2
NT = B // P
NP = NT // 2
FLOPS = 2 * B * D * D * K

X_CHUNKS = [1, 1, 2, 4, 8, 8, 16]
O_CHUNKS = [8, 8, 8, 4, 4, 4, 4]
O_RING = 24


def tile_clusternorm1dv3_t_kernel(tc, x, mu_track, Std_inv_track, out):
    nc = tc.nc
    assert sum(X_CHUNKS) == NT and sum(O_CHUNKS) == NT

    xv = x.rearrange("(p j) e k -> p j (e k)", j=NT)
    ov = out.rearrange("(p j) d k -> p j (d k)", j=NT)
    wv = Std_inv_track.rearrange("k (p c) e -> k p c e", c=T)
    muv = mu_track.rearrange("(t p) k -> t (p k)", t=T)

    with ExitStack() as ctx:
        ctx.enter_context(tc.manual_schedule())
        keep = ctx.enter_context(tc.tile_pool(name="keep", bufs=1))
        rpool = ctx.enter_context(tc.tile_pool(name="rpool", bufs=2))
        gpool = ctx.enter_context(tc.tile_pool(name="gpool", bufs=3))
        cpool = ctx.enter_context(tc.tile_pool(name="cpool", bufs=3))
        psum_t = ctx.enter_context(tc.psum_pool(name="psum_t", bufs=4))
        psum_o = ctx.enter_context(tc.psum_pool(name="psum_o", bufs=4))

        mu_raw = keep.tile([P, P], F32, name="mu_raw")
        nc.gpsimd.memset(mu_raw[:], 0.0)

        x_tiles = []
        x_loads = []
        j0 = 0
        for ci, n in enumerate(X_CHUNKS):
            x_sb = keep.tile([P, n, D * K], BF16, name="x_sb%d" % ci)
            x_loads.append((x_sb, j0, n))
            for jj in range(n):
                x_tiles.append((x_sb, jj))
            j0 += n
        w_sb = [keep.tile([P, T, D], BF16, name="w_sb%d" % k) for k in range(K)]

        def load_x(ci):
            x_sb, a, n = x_loads[ci]
            nc.sync.dma_start(out=x_sb[:], in_=xv[:, a : a + n, :])

        load_x(0)
        nc.sync.dma_start(out=mu_raw[0:T, :].bitcast(BF16), in_=muv)
        load_x(1)
        nc.sync.dma_start(out=w_sb[0][:], in_=wv[0])
        nc.sync.dma_start(out=w_sb[1][:], in_=wv[1])
        for ci in range(2, len(X_CHUNKS)):
            load_x(ci)

        ident_f = keep.tile([P, P], F32, name="ident_f")
        make_identity(nc, ident_f[:])
        ident_b = keep.tile([P, P], BF16, name="ident_b")
        make_identity(nc, ident_b[:])

        w_grp = [keep.tile([P, D, T], BF16, name="w_grp%d" % k, align_bytes=64) for k in range(K)]
        w_codes = keep.tile([P, K, D], U32, name="w_codes", align_bytes=64)
        w_scales = keep.tile([P, K, D], U8, name="w_scales", align_bytes=64)

        mt = psum_t.tile([P, P], F32, name="mt", tag="xt")
        nc.tensor.transpose(mt[:], mu_raw[:], ident_f[:])
        mu_w = keep.tile([P, T], F32, name="mu_w")
        nc.vector.tensor_copy(out=mu_w[:], in_=mt[:, 0:T])
        mu_sb = mu_w[:].bitcast(BF16).rearrange("p (t k) -> p t k", k=K)
        mu_kbt = mu_sb.rearrange("p t k -> p k t").unsqueeze(2).to_broadcast([P, K, P, T])
        mu_tbk = mu_sb.unsqueeze(2).to_broadcast([P, T, P, K])

        xt_of = {}
        xr_of = {}
        xg_of = {}
        xq_of = {}

        def transposes(j):
            x_sb, jj = x_tiles[j]
            words = x_sb[:].bitcast(F32)
            xt = psum_t.tile([P, T, P], F32, name="xt", tag="xt")
            for t in range(T):
                nc.tensor.transpose(xt[:, t, :], words[:, jj, t * P : (t + 1) * P], ident_f[:])
            xt_of[j] = xt

        def pair_tile(n):
            if n not in xg_of:
                xg_of[n] = gpool.tile([P, 2, K, P, T], BF16, name="xg", tag="xg", align_bytes=64)
            return xg_of[n]

        def centre_and_regroup(j):
            nc.vector.tensor_tensor(
                out=pair_tile(j // 2)[:, 1],
                in0=xt_of[j][:].bitcast(BF16).rearrange("p t (b k) -> p k b t", k=K),
                in1=mu_kbt,
                op=ALU.subtract,
            )

        def centre_only(j):
            xr = rpool.tile([P, T, P, K], BF16, name="xr", tag="xr")
            nc.vector.tensor_tensor(
                out=xr[:],
                in0=xt_of[j][:].bitcast(BF16).rearrange("p t (b k) -> p t b k", k=K),
                in1=mu_tbk,
                op=ALU.subtract,
            )
            xr_of[j] = xr

        def regroup(j):
            dst = pair_tile(j // 2)[:, 0]
            src = xr_of[j][:].rearrange("p t b k -> p k b t")
            nc.gpsimd.tensor_scalar(out=dst, in0=src, scalar1=1.0, scalar2=0.0, op0=ALU.mult, op1=ALU.add)

        def quantise(n):
            xc = cpool.tile([P, 2 * K * P], U32, name="xc", tag="xc", align_bytes=64)
            xs = cpool.tile([P, 2 * K * P], U8, name="xs", tag="xs", align_bytes=64)
            nc.vector.quantize_mx(
                out=xc[:].bitcast(FP8X4),
                scales=xs[:],
                in_=xg_of[n][:].rearrange("p s k b t -> p (s k b t)"),
            )
            xq_of[n] = (xc, xs)

        o_ring = keep.tile([P, O_RING, D * K], F32, name="o_ring")
        o_state = {"chunk": 0, "fill": 0, "start": 0}

        def multiply(n):
            xc, xs = xq_of[n]
            banks = []
            for s in range(2):
                po = [psum_o.tile([P, K, H], F32, name="po", tag="po") for h in range(2)]
                for k in range(K):
                    c0 = (s * K + k) * P
                    for h in range(2):
                        nc.tensor.matmul_mx(
                            out=po[h][:, k, :],
                            lhsT=xc[:, c0 : c0 + P].bitcast(FP8X4),
                            lhsT_scale=xs[:, c0 : c0 + P],
                            rhs=w_codes[:, k, h * H : (h + 1) * H].bitcast(FP8X4),
                            rhs_scale=w_scales[:, k, h * H : (h + 1) * H],
                            start=True,
                            stop=True,
                        )
                banks.append(po)
            return banks

        def drain(banks, engines):
            for s in range(2):
                pos = o_state["start"] % O_RING
                jj = pos + o_state["fill"]
                for h in range(2):
                    dst = o_ring[:, jj, h * H * K : (h + 1) * H * K].rearrange("p (d k) -> p d k", k=K)
                    src = banks[s][h][:].rearrange("p k d -> p d k")
                    if engines[s] == "v":
                        nc.vector.tensor_copy(out=dst, in_=src)
                    else:
                        nc.scalar.copy(out=dst, in_=src)
                o_state["fill"] += 1
                n = O_CHUNKS[o_state["chunk"]]
                if o_state["fill"] == n:
                    a = o_state["start"]
                    nc.sync.dma_start(out=ov[:, a : a + n, :], in_=o_ring[:, pos : pos + n, :])
                    o_state["start"] = a + n
                    o_state["chunk"] += 1
                    o_state["fill"] = 0

        def w_transposes(k):
            banks = []
            for cp in range(2):
                wt = psum_o.tile([P, 2, T, P], BF16, name="wt", tag="po")
                for c2 in range(2):
                    for t in range(T):
                        nc.tensor.transpose(
                            wt[:, c2, t, :], w_sb[k][:, 2 * cp + c2, t * P : (t + 1) * P], ident_b[:]
                        )
                banks.append(wt)
            return banks

        def w_copy(k, cp, wt, engine):
            dst = w_grp[k][:].rearrange("p (q a c) t -> p q a (c t)", a=2, c=2)[:, :, cp, :]
            src = wt[:].rearrange("p c t q -> p q (c t)")
            if engine == "v":
                nc.vector.tensor_copy(out=dst, in_=src)
            else:
                nc.scalar.copy(out=dst, in_=src)

        def w_quant(k):
            nc.vector.quantize_mx(
                out=w_codes[:, k, :].bitcast(FP8X4),
                scales=w_scales[:, k, :],
                in_=w_grp[k][:].rearrange("p d t -> p (d t)"),
            )

        transposes(0)
        transposes(1)
        centre_only(0)
        regroup(0)
        wt0 = w_transposes(0)
        centre_and_regroup(1)
        w_copy(0, 0, wt0[0], "v")
        w_copy(0, 1, wt0[1], "v")
        wt1 = w_transposes(1)
        w_copy(1, 0, wt1[0], "s")
        w_copy(1, 1, wt1[1], "s")
        transposes(2)
        transposes(3)
        w_quant(0)
        centre_only(2)
        regroup(2)
        w_quant(1)
        transposes(4)
        transposes(5)
        quantise(0)
        drain(multiply(0), "ss")
        for n in range(1, NP):
            centre_and_regroup(2 * n + 1)
            if n + 1 < NP:
                centre_only(2 * n + 2)
                regroup(2 * n + 2)
            if n + 2 < NP:
                transposes(2 * n + 4)
                transposes(2 * n + 5)
            quantise(n)
            drain(multiply(n), "sv" if n == NP - 1 else "ss")
